import numpy as np
import ml_dtypes


def mxq(x, axis, fmt="e4m3"):
    dtype, down = {"e4m3": (ml_dtypes.float8_e4m3fn, 7), "e5m2": (ml_dtypes.float8_e5m2, 14)}[fmt]
    v = np.moveaxis(np.asarray(x, np.float32).astype(ml_dtypes.bfloat16).astype(np.float64), axis, -1)
    blocks = v.reshape(v.shape[:-1] + (-1, 32))
    amax = np.abs(blocks).max(-1, keepdims=True)
    byte = np.maximum(np.where(amax > 0, np.frexp(amax)[1] - 1 + 127, 0) - down, 1)
    scale = np.exp2(byte - 127.0)
    codes = (blocks / scale).astype(np.float32).astype(dtype).astype(np.float64)
    return np.moveaxis((codes * scale).reshape(v.shape), -1, axis)


WIDE = False


def mx_kscale(k):
    if not WIDE:
        return np.ones(k)
    levels = np.array([10, -10, 5, -5, 0])
    a = np.random.permutation(np.resize(levels, k // 512 * 4)).reshape(k // 512, 4)
    idx = np.arange(k)
    return np.exp2(a[idx // 512, idx % 128 // 32])


BF16 = ml_dtypes.bfloat16


def bf(x):
    return np.asarray(x, np.float32).astype(BF16)


def f64(x):
    return np.asarray(x).astype(np.float64)


E2M1 = np.array([0.0, 0.5, 1.0, 1.5, 2.0, 3.0, 4.0, 6.0, -0.0, -0.5, -1.0, -1.5, -2.0, -3.0, -4.0, -6.0])


def pack_weight(w, fmt):
    k, n = w.shape
    w = f64(bf(w)).reshape(k // 32, 32, n)
    amax = np.abs(w).max(1)
    if fmt == "e4m3":
        byte = np.frexp(amax)[1] - 1 + 127 - 7
    else:
        mant, ex = np.frexp(amax / 6.0)
        byte = np.where(mant > 0.5, ex, ex - 1) + 127
    byte = np.clip(np.where(amax > 0, byte, 1), 1, 254)
    scaled = (w * np.exp2(127.0 - byte)[:, None, :]).reshape(k, n).astype(np.float32)
    by_word = np.ascontiguousarray(scaled.reshape(k // 512, 128, 4, n).transpose(0, 1, 3, 2))
    if fmt == "e4m3":
        words = by_word.astype(ml_dtypes.float8_e4m3fn).view(np.uint8)
    else:
        c = by_word.astype(ml_dtypes.float4_e2m1fn).view(np.uint8) & 0xF
        words = c[..., 0::2] | (c[..., 1::2] << 4)
    return np.ascontiguousarray(words), np.ascontiguousarray(byte.astype(np.uint8).reshape(k // 512, 16, n))


def unpack_weight(words, scales, fmt):
    g, p, n, _ = words.shape
    if fmt == "e4m3":
        vals = np.ascontiguousarray(words).view(ml_dtypes.float8_e4m3fn).astype(np.float64)
    else:
        nib = np.empty((g, p, n, 4), np.uint8)
        nib[..., 0::2] = words & 0xF
        nib[..., 1::2] = words >> 4
        vals = E2M1[nib]
    vals = vals * np.repeat(np.exp2(scales.astype(np.float64) - 127.0), 8, axis=1)[..., None]
    return vals.transpose(0, 1, 3, 2).reshape(g * 512, n)


G, GI, GO, B = 32, 512, 32, 128
K = G * GI
N = G * GO


def build_mask():
    mask = np.ones((N, K))
    for g in range(G):
        mask[g * GO:(g + 1) * GO, g * GI:(g + 1) * GI] = 0.0
    return mask


def setup_inputs():
    s = mx_kscale(K)
    bound = 1.0 / np.sqrt(K)
    W = np.random.uniform(-bound, bound, (N, K)) * build_mask()
    data = bf(np.random.standard_normal((B, K)) * s)
    words, scales = pack_weight((W / s[None, :]).T, "e4m3")
    return {"data": data,
            "W_words": words,
            "W_scales": scales,
            "b": bf(np.random.standard_normal(N) * 0.3)}


def reference(data, W_words, W_scales, b):
    return (mxq(f64(data), 1, "e4m3") @ unpack_weight(W_words, W_scales, "e4m3")) + f64(b)

@@ -1,0 +1,127 @@
+import concourse.mybir as mybir
+from concourse.masks import make_identity
+
+F32 = mybir.dt.float32
+BF16 = mybir.dt.bfloat16
+I32 = mybir.dt.int32
+U32 = mybir.dt.uint32
+U8 = mybir.dt.uint8
+FP8X4 = mybir.dt.float8_e4m3fn_x4
+
+P = 128
+PACK = 4
+K_PASS = P * PACK
+WORDS_PASS = K_PASS // 2
+
+ROWS = 128
+K = 16384
+N = 1024
+PASSES = K // K_PASS
+N_TILE = 512
+N_TILES = N // N_TILE
+
+QUADRANTS = 4
+SCALE_ROWS = 4
+SHARE = 4
+PLANES = PASSES // SHARE
+
+DATA_LOADS = 4
+PAIR = 2
+
+FLOPS = 2 * ROWS * K * N
+
+
+def tile_groupfc_k_kernel(tc, data, W_words, W_scales, b, out):
+    nc = tc.nc
+    with (
+        tc.tile_pool(name="keep", bufs=1) as keep,
+        tc.tile_pool(name="stage", bufs=4) as stage,
+        tc.psum_pool(name="turned", bufs=4) as turned_pool,
+        tc.psum_pool(name="bias", bufs=1) as bias_pool,
+        tc.psum_pool(name="sums", bufs=1) as sums_pool,
+    ):
+        x_sb = keep.tile([P, K], BF16)
+        w_words = keep.tile([P, PASSES, N], U32, align_bytes=64)
+        w_planes = keep.tile([P, PLANES, N], U8, align_bytes=64)
+        x_codes = keep.tile([P, PASSES, ROWS], U32, align_bytes=64)
+        x_scales = keep.tile([P, PASSES, ROWS], U8, align_bytes=64)
+        result = keep.tile([P, N], F32)
+
+        nc.vector.memset(w_planes[:].rearrange("p s n -> p (s n)").bitcast(I32), 0)
+
+        cols_load = K // DATA_LOADS
+        for c in range(DATA_LOADS):
+            k_cols = slice(c * cols_load, (c + 1) * cols_load)
+            nc.sync.dma_start(out=x_sb[:, k_cols], in_=data[:, k_cols])
+
+        for s in range(PLANES):
+            for quad in range(QUADRANTS):
+                first = 32 * quad
+                nc.sync.dma_start(
+                    out=w_planes[first : first + SHARE * SCALE_ROWS, s, :].bitcast(I32),
+                    in_=W_scales[
+                        SHARE * s : SHARE * (s + 1), SCALE_ROWS * quad : SCALE_ROWS * (quad + 1), :
+                    ].bitcast(I32),
+                )
+
+        for g in range(PASSES):
+            nc.sync.dma_start(
+                out=w_words[:, g, :].bitcast(I32),
+                in_=W_words[g].rearrange("p n t -> p (n t)").bitcast(I32),
+            )
+
+        ones = keep.tile([P, P], BF16)
+        nc.vector.memset(ones[:], 1.0)
+        bias_rows = keep.tile([P, N], BF16)
+        nc.vector.memset(bias_rows[:], 0.0)
+        nc.scalar.dma_start(out=bias_rows[0:1, :], in_=b.rearrange("(o n) -> o n", o=1))
+        for h in range(N_TILES):
+            n_cols = slice(h * N_TILE, (h + 1) * N_TILE)
+            bias_bank = bias_pool.tile([P, N_TILE], F32)
+            nc.tensor.matmul(out=bias_bank[:], lhsT=ones[:], rhs=bias_rows[:, n_cols], start=True, stop=True)
+            nc.scalar.copy(out=result[:, n_cols], in_=bias_bank[:])
+
+        identity = keep.tile([P, P], F32)
+        make_identity(nc, identity[:])
+        x_words = x_sb[:].bitcast(F32)
+        for pair in range(PASSES // PAIR):
+            turned = turned_pool.tile([P, PAIR, 2, ROWS], F32)
+            for i in range(PAIR):
+                first_word = (PAIR * pair + i) * WORDS_PASS
+                for u in range(2):
+                    nc.tensor.transpose(
+                        turned[:, i, u, :],
+                        x_words[:, first_word + u : first_word + WORDS_PASS : 2],
+                        identity[:],
+                    )
+            grouped = stage.tile([P, PAIR, ROWS, PACK], BF16, align_bytes=64)
+            copy = nc.vector.tensor_copy if pair % 2 == 0 else nc.scalar.copy
+            copy(out=grouped[:].bitcast(F32), in_=turned[:].rearrange("p i u r -> p i r u"))
+            both = slice(PAIR * pair, PAIR * (pair + 1))
+            nc.vector.quantize_mx(
+                out=x_codes[:, both, :].rearrange("p g r -> p (g r)").bitcast(FP8X4),
+                scales=x_scales[:, both, :].rearrange("p g r -> p (g r)"),
+                in_=grouped[:].rearrange("p i r t -> p (i r t)"),
+            )
+
+        sums = [sums_pool.tile([P, N_TILE], F32, name="sums%d" % h) for h in range(N_TILES)]
+        for g in range(PASSES):
+            s, j = divmod(g, SHARE)
+            for h in range(N_TILES):
+                n_cols = slice(h * N_TILE, (h + 1) * N_TILE)
+                nc.tensor.matmul_mx(
+                    out=sums[h][:],
+                    lhsT=x_codes[:, g, :].bitcast(FP8X4),
+                    lhsT_scale=x_scales[:, g, :],
+                    rhs=w_words[:, g, n_cols].bitcast(FP8X4),
+                    rhs_scale=w_planes[SCALE_ROWS * j : P, s, n_cols],
+                    start=(g == 0),
+                    stop=(g == PASSES - 1),
+                )
+
+        for h in range(N_TILES):
+            n_cols = slice(h * N_TILE, (h + 1) * N_TILE)
+            nc.vector.tensor_tensor(
+                out=result[:, n_cols], in0=sums[h][:], in1=result[:, n_cols], op=mybir.AluOpType.add
+            )
+            nc.sync.dma_start(out=out[:, n_cols], in_=result[:, n_cols])

@@ -47,34 +47,11 @@ def tile_groupfc_k_kernel(tc, data, W_words, W_scales, b, out):
         x_scales = keep.tile([P, PASSES, ROWS], U8, align_bytes=64)
         result = keep.tile([P, N], F32)
 
-        nc.vector.memset(w_planes[:].rearrange("p s n -> p (s n)").bitcast(I32), 0)
-
-        cols_load = K // DATA_LOADS
-        for c in range(DATA_LOADS):
-            k_cols = slice(c * cols_load, (c + 1) * cols_load)
-            nc.sync.dma_start(out=x_sb[:, k_cols], in_=data[:, k_cols])
-
-        for s in range(PLANES):
-            for quad in range(QUADRANTS):
-                first = 32 * quad
-                nc.sync.dma_start(
-                    out=w_planes[first : first + SHARE * SCALE_ROWS, s, :].bitcast(I32),
-                    in_=W_scales[
-                        SHARE * s : SHARE * (s + 1), SCALE_ROWS * quad : SCALE_ROWS * (quad + 1), :
-                    ].bitcast(I32),
-                )
-
-        for g in range(PASSES):
-            nc.sync.dma_start(
-                out=w_words[:, g, :].bitcast(I32),
-                in_=W_words[g].rearrange("p n t -> p (n t)").bitcast(I32),
-            )
-
-        ones = keep.tile([P, P], BF16)
-        nc.vector.memset(ones[:], 1.0)
         bias_rows = keep.tile([P, N], BF16)
         nc.vector.memset(bias_rows[:], 0.0)
-        nc.scalar.dma_start(out=bias_rows[0:1, :], in_=b.rearrange("(o n) -> o n", o=1))
+        nc.sync.dma_start(out=bias_rows[0:1, :], in_=b.rearrange("(o n) -> o n", o=1))
+        ones = keep.tile([P, P], BF16)
+        nc.vector.memset(ones[:], 1.0)
         for h in range(N_TILES):
             n_cols = slice(h * N_TILE, (h + 1) * N_TILE)
             bias_bank = bias_pool.tile([P, N_TILE], F32)
@@ -83,6 +60,30 @@ def tile_groupfc_k_kernel(tc, data, W_words, W_scales, b, out):
 
         identity = keep.tile([P, P], F32)
         make_identity(nc, identity[:])
+
+        nc.vector.memset(w_planes[:].rearrange("p s n -> p (s n)").bitcast(I32), 0)
+
+        cols_load = K // DATA_LOADS
+        for c in range(DATA_LOADS):
+            k_cols = slice(c * cols_load, (c + 1) * cols_load)
+            nc.sync.dma_start(out=x_sb[:, k_cols], in_=data[:, k_cols])
+
+        for g in range(PASSES):
+            nc.sync.dma_start(
+                out=w_words[:, g, :].bitcast(I32),
+                in_=W_words[g].rearrange("p n t -> p (n t)").bitcast(I32),
+            )
+
+        for s in range(PLANES):
+            for quad in range(QUADRANTS):
+                first = 32 * quad
+                nc.gpsimd.dma_start(
+                    out=w_planes[first : first + SHARE * SCALE_ROWS, s, :].bitcast(F32),
+                    in_=W_scales[
+                        SHARE * s : SHARE * (s + 1), SCALE_ROWS * quad : SCALE_ROWS * (quad + 1), :
+                    ].bitcast(F32),
+                )
+
         x_words = x_sb[:].bitcast(F32)
         for pair in range(PASSES // PAIR):
             turned = turned_pool.tile([P, PAIR, 2, ROWS], F32)

@@ -66,7 +66,7 @@ def tile_groupfc_k_kernel(tc, data, W_words, W_scales, b, out):
         cols_load = K // DATA_LOADS
         for c in range(DATA_LOADS):
             k_cols = slice(c * cols_load, (c + 1) * cols_load)
-            nc.sync.dma_start(out=x_sb[:, k_cols], in_=data[:, k_cols])
+            nc.scalar.dma_start(out=x_sb[:, k_cols], in_=data[:, k_cols])
 
         for g in range(PASSES):
             nc.sync.dma_start(

@@ -26,6 +26,7 @@ SHARE = 4
 PLANES = PASSES // SHARE
 
 DATA_LOADS = 4
+LAST = 2
 PAIR = 2
 
 FLOPS = 2 * ROWS * K * N
@@ -68,11 +69,18 @@ def tile_groupfc_k_kernel(tc, data, W_words, W_scales, b, out):
             k_cols = slice(c * cols_load, (c + 1) * cols_load)
             nc.scalar.dma_start(out=x_sb[:, k_cols], in_=data[:, k_cols])
 
-        for g in range(PASSES):
+        for g in range(PASSES - LAST):
             nc.sync.dma_start(
                 out=w_words[:, g, :].bitcast(I32),
                 in_=W_words[g].rearrange("p n t -> p (n t)").bitcast(I32),
             )
+        for h in range(N_TILES):
+            n_cols = slice(h * N_TILE, (h + 1) * N_TILE)
+            for g in range(PASSES - LAST, PASSES):
+                nc.sync.dma_start(
+                    out=w_words[:, g, n_cols].bitcast(I32),
+                    in_=W_words[g, :, n_cols, :].rearrange("p n t -> p (n t)").bitcast(I32),
+                )
 
         for s in range(PLANES):
             for quad in range(QUADRANTS):
@@ -106,22 +114,28 @@ def tile_groupfc_k_kernel(tc, data, W_words, W_scales, b, out):
             )
 
         sums = [sums_pool.tile([P, N_TILE], F32, name="sums%d" % h) for h in range(N_TILES)]
-        for g in range(PASSES):
+
+        def multiply(g, h):
             s, j = divmod(g, SHARE)
+            n_cols = slice(h * N_TILE, (h + 1) * N_TILE)
+            nc.tensor.matmul_mx(
+                out=sums[h][:],
+                lhsT=x_codes[:, g, :].bitcast(FP8X4),
+                lhsT_scale=x_scales[:, g, :],
+                rhs=w_words[:, g, n_cols].bitcast(FP8X4),
+                rhs_scale=w_planes[SCALE_ROWS * j : P, s, n_cols],
+                start=(g == 0),
+                stop=(g == PASSES - 1),
+            )
+
+        for g in range(PASSES - LAST):
             for h in range(N_TILES):
-                n_cols = slice(h * N_TILE, (h + 1) * N_TILE)
-                nc.tensor.matmul_mx(
-                    out=sums[h][:],
-                    lhsT=x_codes[:, g, :].bitcast(FP8X4),
-                    lhsT_scale=x_scales[:, g, :],
-                    rhs=w_words[:, g, n_cols].bitcast(FP8X4),
-                    rhs_scale=w_planes[SCALE_ROWS * j : P, s, n_cols],
-                    start=(g == 0),
-                    stop=(g == PASSES - 1),
-                )
+                multiply(g, h)
 
         for h in range(N_TILES):
             n_cols = slice(h * N_TILE, (h + 1) * N_TILE)
+            for g in range(PASSES - LAST, PASSES):
+                multiply(g, h)
             nc.vector.tensor_tensor(
                 out=result[:, n_cols], in0=sums[h][:], in1=result[:, n_cols], op=mybir.AluOpType.add
             )

@@ -19,13 +19,13 @@ N = 1024
 PASSES = K // K_PASS
 N_TILE = 512
 N_TILES = N // N_TILE
+RANGES = (slice(0, 512), slice(512, 768), slice(768, 1024))
 
 QUADRANTS = 4
 SCALE_ROWS = 4
 SHARE = 4
 PLANES = PASSES // SHARE
 
-DATA_LOADS = 4
 LAST = 2
 PAIR = 2
 
@@ -64,23 +64,21 @@ def tile_groupfc_k_kernel(tc, data, W_words, W_scales, b, out):
 
         nc.vector.memset(w_planes[:].rearrange("p s n -> p (s n)").bitcast(I32), 0)
 
-        cols_load = K // DATA_LOADS
-        for c in range(DATA_LOADS):
-            k_cols = slice(c * cols_load, (c + 1) * cols_load)
-            nc.scalar.dma_start(out=x_sb[:, k_cols], in_=data[:, k_cols])
+        nc.scalar.dma_start(out=x_sb[:], in_=data)
 
         for g in range(PASSES - LAST):
             nc.sync.dma_start(
                 out=w_words[:, g, :].bitcast(I32),
                 in_=W_words[g].rearrange("p n t -> p (n t)").bitcast(I32),
             )
-        for h in range(N_TILES):
-            n_cols = slice(h * N_TILE, (h + 1) * N_TILE)
-            for g in range(PASSES - LAST, PASSES):
-                nc.sync.dma_start(
-                    out=w_words[:, g, n_cols].bitcast(I32),
-                    in_=W_words[g, :, n_cols, :].rearrange("p n t -> p (n t)").bitcast(I32),
-                )
+        tail = [(g, slice(0, 512)) for g in range(PASSES - LAST, PASSES)]
+        tail += [(g, slice(512, 1024)) for g in range(PASSES - LAST, PASSES - 1)]
+        tail += [(PASSES - 1, n_cols) for n_cols in RANGES[1:]]
+        for g, n_cols in tail:
+            nc.sync.dma_start(
+                out=w_words[:, g, n_cols].bitcast(I32),
+                in_=W_words[g, :, n_cols, :].rearrange("p n t -> p (n t)").bitcast(I32),
+            )
 
         for s in range(PLANES):
             for quad in range(QUADRANTS):
@@ -113,30 +111,39 @@ def tile_groupfc_k_kernel(tc, data, W_words, W_scales, b, out):
                 in_=grouped[:].rearrange("p i r t -> p (i r t)"),
             )
 
-        sums = [sums_pool.tile([P, N_TILE], F32, name="sums%d" % h) for h in range(N_TILES)]
+        sums = [sums_pool.tile([P, N_TILE], F32, name="sums%d" % c) for c in range(len(RANGES))]
 
-        def multiply(g, h):
+        def multiply(g, c):
             s, j = divmod(g, SHARE)
-            n_cols = slice(h * N_TILE, (h + 1) * N_TILE)
             nc.tensor.matmul_mx(
-                out=sums[h][:],
+                out=sums[c][:, : RANGES[c].stop - RANGES[c].start],
                 lhsT=x_codes[:, g, :].bitcast(FP8X4),
                 lhsT_scale=x_scales[:, g, :],
-                rhs=w_words[:, g, n_cols].bitcast(FP8X4),
-                rhs_scale=w_planes[SCALE_ROWS * j : P, s, n_cols],
+                rhs=w_words[:, g, RANGES[c]].bitcast(FP8X4),
+                rhs_scale=w_planes[SCALE_ROWS * j : P, s, RANGES[c]],
                 start=(g == 0),
                 stop=(g == PASSES - 1),
             )
 
-        for g in range(PASSES - LAST):
-            for h in range(N_TILES):
-                multiply(g, h)
-
-        for h in range(N_TILES):
-            n_cols = slice(h * N_TILE, (h + 1) * N_TILE)
-            for g in range(PASSES - LAST, PASSES):
-                multiply(g, h)
+        def finish(c, queue):
             nc.vector.tensor_tensor(
-                out=result[:, n_cols], in0=sums[h][:], in1=result[:, n_cols], op=mybir.AluOpType.add
+                out=result[:, RANGES[c]],
+                in0=sums[c][:, : RANGES[c].stop - RANGES[c].start],
+                in1=result[:, RANGES[c]],
+                op=mybir.AluOpType.add,
             )
-            nc.sync.dma_start(out=out[:, n_cols], in_=result[:, n_cols])
+            queue.dma_start(out=out[:, RANGES[c]], in_=result[:, RANGES[c]])
+
+        for g in range(PASSES - LAST):
+            for c in range(len(RANGES)):
+                multiply(g, c)
+
+        for g in range(PASSES - LAST, PASSES):
+            multiply(g, 0)
+        finish(0, nc.sync)
+        for g in range(PASSES - LAST, PASSES - 1):
+            for c in (1, 2):
+                multiply(g, c)
+        for c, queue in ((1, nc.scalar), (2, nc.sync)):
+            multiply(PASSES - 1, c)
+            finish(c, queue)

import concourse.mybir as mybir
from concourse.masks import make_identity

F32 = mybir.dt.float32
BF16 = mybir.dt.bfloat16
I32 = mybir.dt.int32
U32 = mybir.dt.uint32
U8 = mybir.dt.uint8
FP8X4 = mybir.dt.float8_e4m3fn_x4

P = 128
PACK = 4
K_PASS = P * PACK
WORDS_PASS = K_PASS // 2

ROWS = 128
K = 16384
N = 1024
PASSES = K // K_PASS
N_TILE = 512
N_TILES = N // N_TILE
RANGES = (slice(0, 512), slice(512, 768), slice(768, 1024))

QUADRANTS = 4
SCALE_ROWS = 4
SHARE = 4
PLANES = PASSES // SHARE

LAST = 2
PAIR = 2

FLOPS = 2 * ROWS * K * N


def tile_groupfc_k_kernel(tc, data, W_words, W_scales, b, out):
    nc = tc.nc
    with (
        tc.tile_pool(name="keep", bufs=1) as keep,
        tc.tile_pool(name="stage", bufs=4) as stage,
        tc.psum_pool(name="turned", bufs=4) as turned_pool,
        tc.psum_pool(name="bias", bufs=1) as bias_pool,
        tc.psum_pool(name="sums", bufs=1) as sums_pool,
    ):
        x_sb = keep.tile([P, K], BF16)
        w_words = keep.tile([P, PASSES, N], U32, align_bytes=64)
        w_planes = keep.tile([P, PLANES, N], U8, align_bytes=64)
        x_codes = keep.tile([P, PASSES, ROWS], U32, align_bytes=64)
        x_scales = keep.tile([P, PASSES, ROWS], U8, align_bytes=64)
        result = keep.tile([P, N], F32)

        bias_rows = keep.tile([P, N], BF16)
        nc.vector.memset(bias_rows[:], 0.0)
        nc.sync.dma_start(out=bias_rows[0:1, :], in_=b.rearrange("(o n) -> o n", o=1))
        ones = keep.tile([P, P], BF16)
        nc.vector.memset(ones[:], 1.0)
        for h in range(N_TILES):
            n_cols = slice(h * N_TILE, (h + 1) * N_TILE)
            bias_bank = bias_pool.tile([P, N_TILE], F32)
            nc.tensor.matmul(out=bias_bank[:], lhsT=ones[:], rhs=bias_rows[:, n_cols], start=True, stop=True)
            nc.scalar.copy(out=result[:, n_cols], in_=bias_bank[:])

        identity = keep.tile([P, P], F32)
        make_identity(nc, identity[:])

        nc.vector.memset(w_planes[:].rearrange("p s n -> p (s n)").bitcast(I32), 0)

        nc.scalar.dma_start(out=x_sb[:], in_=data)

        for g in range(PASSES - LAST):
            nc.sync.dma_start(
                out=w_words[:, g, :].bitcast(I32),
                in_=W_words[g].rearrange("p n t -> p (n t)").bitcast(I32),
            )
        tail = [(g, slice(0, 512)) for g in range(PASSES - LAST, PASSES)]
        tail += [(g, slice(512, 1024)) for g in range(PASSES - LAST, PASSES - 1)]
        tail += [(PASSES - 1, n_cols) for n_cols in RANGES[1:]]
        for g, n_cols in tail:
            nc.sync.dma_start(
                out=w_words[:, g, n_cols].bitcast(I32),
                in_=W_words[g, :, n_cols, :].rearrange("p n t -> p (n t)").bitcast(I32),
            )

        for s in range(PLANES):
            for quad in range(QUADRANTS):
                first = 32 * quad
                nc.gpsimd.dma_start(
                    out=w_planes[first : first + SHARE * SCALE_ROWS, s, :].bitcast(F32),
                    in_=W_scales[
                        SHARE * s : SHARE * (s + 1), SCALE_ROWS * quad : SCALE_ROWS * (quad + 1), :
                    ].bitcast(F32),
                )

        x_words = x_sb[:].bitcast(F32)
        for pair in range(PASSES // PAIR):
            turned = turned_pool.tile([P, PAIR, 2, ROWS], F32)
            for i in range(PAIR):
                first_word = (PAIR * pair + i) * WORDS_PASS
                for u in range(2):
                    nc.tensor.transpose(
                        turned[:, i, u, :],
                        x_words[:, first_word + u : first_word + WORDS_PASS : 2],
                        identity[:],
                    )
            grouped = stage.tile([P, PAIR, ROWS, PACK], BF16, align_bytes=64)
            copy = nc.vector.tensor_copy if pair % 2 == 0 else nc.scalar.copy
            copy(out=grouped[:].bitcast(F32), in_=turned[:].rearrange("p i u r -> p i r u"))
            both = slice(PAIR * pair, PAIR * (pair + 1))
            nc.vector.quantize_mx(
                out=x_codes[:, both, :].rearrange("p g r -> p (g r)").bitcast(FP8X4),
                scales=x_scales[:, both, :].rearrange("p g r -> p (g r)"),
                in_=grouped[:].rearrange("p i r t -> p (i r t)"),
            )

        sums = [sums_pool.tile([P, N_TILE], F32, name="sums%d" % c) for c in range(len(RANGES))]

        def multiply(g, c):
            s, j = divmod(g, SHARE)
            nc.tensor.matmul_mx(
                out=sums[c][:, : RANGES[c].stop - RANGES[c].start],
                lhsT=x_codes[:, g, :].bitcast(FP8X4),
                lhsT_scale=x_scales[:, g, :],
                rhs=w_words[:, g, RANGES[c]].bitcast(FP8X4),
                rhs_scale=w_planes[SCALE_ROWS * j : P, s, RANGES[c]],
                start=(g == 0),
                stop=(g == PASSES - 1),
            )

        def finish(c, queue):
            nc.vector.tensor_tensor(
                out=result[:, RANGES[c]],
                in0=sums[c][:, : RANGES[c].stop - RANGES[c].start],
                in1=result[:, RANGES[c]],
                op=mybir.AluOpType.add,
            )
            queue.dma_start(out=out[:, RANGES[c]], in_=result[:, RANGES[c]])

        for g in range(PASSES - LAST):
            for c in range(len(RANGES)):
                multiply(g, c)

        for g in range(PASSES - LAST, PASSES):
            multiply(g, 0)
        finish(0, nc.sync)
        for g in range(PASSES - LAST, PASSES - 1):
            for c in (1, 2):
                multiply(g, c)
        for c, queue in ((1, nc.scalar), (2, nc.sync)):
            multiply(PASSES - 1, c)
            finish(c, queue)
